import numpy as np
import ml_dtypes


def mxq(x, axis, fmt="e4m3"):
    dtype, down = {"e4m3": (ml_dtypes.float8_e4m3fn, 7), "e5m2": (ml_dtypes.float8_e5m2, 14)}[fmt]
    v = np.moveaxis(np.asarray(x, np.float32).astype(ml_dtypes.bfloat16).astype(np.float64), axis, -1)
    blocks = v.reshape(v.shape[:-1] + (-1, 32))
    amax = np.abs(blocks).max(-1, keepdims=True)
    byte = np.maximum(np.where(amax > 0, np.frexp(amax)[1] - 1 + 127, 0) - down, 1)
    scale = np.exp2(byte - 127.0)
    codes = (blocks / scale).astype(np.float32).astype(dtype).astype(np.float64)
    return np.moveaxis((codes * scale).reshape(v.shape), -1, axis)


WIDE = False


def mx_kscale(k):
    if not WIDE:
        return np.ones(k)
    levels = np.array([18, -18])
    if k % 512:
        return np.exp2(np.random.permutation(np.resize(levels, k // 32))).repeat(32)
    a = np.empty((k // 512, 16))
    for p in range(k // 512):
        a[p, :8] = np.random.permutation(np.resize(levels, 8))
        for g in range(8):
            far = levels[np.abs(levels - a[p, g]) >= 10]
            a[p, g + 8] = far[np.random.randint(len(far))]
    return np.exp2(a.ravel()).repeat(32)


BF16 = ml_dtypes.bfloat16


def bf(x):
    return np.asarray(x, np.float32).astype(BF16)


def f64(x):
    return np.asarray(x).astype(np.float64)


SL, BS, DM, H, NH, DO = 4, 512, 1024, 16, 64, 1024
DP = H * NH
T = BS * SL


def setup_inputs():
    s = mx_kscale(T).reshape(BS, SL)
    u = mx_kscale(DO)
    v = mx_kscale(DP)
    g = np.random.standard_normal((SL, BS, H)) * 2.0
    x0 = bf(np.random.standard_normal((SL, BS, DM)))
    logw = bf(g - np.log(np.exp(g).sum(0, keepdims=True)))
    wv0 = bf(np.random.standard_normal((DP, DM)) / np.sqrt(DM * SL))
    wo0 = bf(np.random.standard_normal((DO, DP)) * 0.5 / np.sqrt(DP))
    go = bf(np.random.standard_normal((BS, DO)) * np.exp2(np.random.randint(-6, 1, (BS, 1))) * 2.0 / s[:, :1] * u)
    pool_w = f64(logw)
    return {"values": bf(f64(x0) * s.T[:, :, None]),
            "logw": logw,
            "Wv": bf(f64(wv0) / v[:, None]),
            "Wo": bf(f64(wo0) * v[None, :] / u[:, None]),
            "pool_w": np.asarray(pool_w, np.float32),
            "grad_out": go}


def reference(values, logw, Wv, Wo, pool_w, grad_out):
    dattn = mxq(f64(grad_out), 1, "e5m2") @ mxq(f64(Wo), 0, "e4m3")
    pw = f64(pool_w).transpose(1, 0, 2)
    dvp = (pw[..., None] * dattn.reshape(BS, 1, H, NH)).reshape(T, DP)
    dx = mxq(dvp, 1, "e5m2") @ mxq(f64(Wv), 0, "e4m3")
    dvalues = dx.reshape(BS, SL, DM).transpose(1, 0, 2)
    xt = f64(values).transpose(1, 0, 2).reshape(T, DM)
    dWv = mxq(dvp, 0, "e5m2").T @ mxq(xt, 0, "e4m3")
    return dvalues, dWv

@@ -1,0 +1,271 @@
+from contextlib import ExitStack
+
+import concourse.mybir as mybir
+from concourse.masks import make_identity
+
+FLOPS = 2 * 512 * 1024 * 1024 + 2 * 2 * 2048 * 1024 * 1024
+BYTES = 2 * (4 * 512 * 1024 + 2 * 1024 * 1024 + 512 * 1024) + 4 * 4 * 512 * 16 + 4 * (2048 * 1024 + 1024 * 1024)
+
+F32 = mybir.dt.float32
+BF16 = mybir.dt.bfloat16
+U32 = mybir.dt.uint32
+U8 = mybir.dt.uint8
+E4 = mybir.dt.float8_e4m3fn_x4
+E5 = mybir.dt.float8_e5m2_x4
+MULT = mybir.AluOpType.mult
+P = 128
+
+ORDER = """
+Lgo0:D LWo00:D GT0:P GC0:V LWo10:D WoI001:S WoI000:V GQ0:V LWo01:D WoI010:S WoI011:V WoQ00:V LWo11:D WoI100:S
+WoQ01:V Lpw:D WoI101:V DA00:P WoI110:S Lgo1:D WoQ10:V LX0:D GT1:P M00:V WoI111:S GC1:S LWv0:D XI00:S WoQ11:V
+TT000:P DQ00:V DA01:P TC000:S GQ1:V TT001:P XI01:V Lgo2:D M01:V XI02:S LWv1:D WvI00:S WvI01:V TT010:P TC001:S
+LX1:D WvI11:V WvQ00:V TC010:S TT011:P XQ00:V DA10:P XI03:S WvI02:V Lgo3:D GT2:P LX2:D WvI03:V GC2:S M10:V
+WvI10:S LX3:D XI10:S GQ2:V DA11:P XQ01:V XI11:S WvI12:V WvQ10:V TC011:S WvQ01:V TQ00:V XI12:S TT100:P TQ01:V
+GT3:P M11:V TC100:S O0_000:P XI21:S TT101:P XQ10:V DA20:P GC3:S WvI13:V TC101:S TT110:P DQ01:V WvQ11:V E0_000:S
+XI13:V XI22:S O0_001:P M20:V O0_010:P TC110:S O0_011:P TT111:P E0_001:S O0_020:P DQ10:V TC111:S DA21:P S0_00:D
+TQ10:V O0_021:P E0_010:S DQ11:V O0_030:P E0_011:S TQ11:V O0_031:P E0_020:S M21:V TT200:P S0_01:D E0_021:S
+TT201:P TC200:S S0_02:D O0_100:P XI23:S XQ11:V GQ3:V XI20:V E0_030:S DA30:P DQ20:V XI30:S O1_0000:P O1_0001:P
+M30:V TT210:P O0_101:P E0_031:S XI31:S DQ21:V E0_100:S DA31:P XQ20:V O0_110:P TC201:S DQ30:V O0_111:P XQ21:V
+TC210:S O1_0002:P TT211:P XQ30:V XI32:S TC211:V O1_0003:P O1_0010:P O1_0011:P TT300:P XI33:V E1_000:S O1_0012:P
+E0_101:S XQ31:V O0_120:P E0_110:S TQ20:V O0_121:P E0_111:S TC300:V O1_0013:P O1_0100:P E1_001:S O1_0101:P
+O1_0102:P E0_120:S M31:V O0_130:P S1_00:D E0_121:S O0_131:P O1_0103:P S0_03:D O1_0110:P TT301:P E1_010:V
+O1_0111:P S0_10:D E0_130:S TT310:P TQ21:V TC301:S O1_0112:P DQ31:V S0_11:D O1_0113:P O0_200:P TC310:V E0_131:S
+O1_0200:P O1_0201:P E0_200:S O1_0202:P E1_011:V O1_0203:P O1_0210:P E1_020:S O1_0211:P S1_01:D O1_0212:P
+O1_0213:P O0_201:P E1_021:S O0_210:P E0_201:S S1_02:D TT311:P O1_0300:P TC311:V O1_0301:P S0_12:D O1_0302:P
+O1_0303:P O1_0310:P E0_210:V E1_030:S O0_211:P S0_13:D O1_0311:P E0_211:S O1_0312:P O1_0313:P O0_220:P E1_031:V
+O1_1000:P E0_220:V O1_1001:P S1_03:D O0_221:P O1_1002:P E0_221:V O0_230:P S0_20:D O1_1003:P E0_230:V O1_1010:P
+O1_1011:P S0_21:D E1_100:V O0_231:P TQ30:V O1_1012:P O1_1013:P TQ31:V O1_1100:P E1_101:S O1_1101:P O1_1102:P
+E0_231:S O0_300:P S1_10:D O0_301:P E0_300:V O1_1103:P S0_22:D E0_301:S O1_1110:P E1_110:V O0_310:P O1_1111:P
+S0_23:D E0_310:S O0_311:P O1_1112:P E0_311:S O1_1113:P O1_1200:P E1_111:V O1_1201:P O0_320:P S1_11:D O1_1202:P
+E0_320:S O1_1203:P O1_1210:P E1_120:V O1_1211:P S0_30:D O1_1212:P O0_321:P O0_330:P S0_31:D E0_321:S O1_1213:P
+O0_331:P E1_121:S S0_32:D O1_1300:P E0_330:S O1_1301:P O1_1302:P E0_331:S O1_1303:P S1_12:D O1_1310:P E1_130:S
+O1_1311:P O1_1312:P O1_1313:P S0_33:D E1_131:S S1_13:D
+"""
+
+
+def tile_multiheadattention_pb_v_kernel(tc, values, logw, Wv, Wo, pool_w, grad_out, out_0, out_1):
+    nc = tc.nc
+    with ExitStack() as ctx:
+        keep = ctx.enter_context(tc.tile_pool(name="keep", bufs=1))
+        work = ctx.enter_context(tc.tile_pool(name="work", bufs=1))
+        psum = ctx.enter_context(tc.psum_pool(name="psum", bufs=1))
+
+        ident = keep.tile([P, P], F32, name="ident")
+        make_identity(nc, ident[:])
+        pw = keep.tile([P, 4, 4, 16], F32, name="pw")
+        go_raw = [keep.tile([P, 1024], BF16, name="go_raw%d" % i) for i in range(4)]
+        goq = keep.tile([P, 4, 2, P], U32, name="goq", align_bytes=64)
+        gos = keep.tile([P, 4, 2, P], U8, name="gos", align_bytes=64)
+        woq = keep.tile([P, 2, 1024], U32, name="woq", align_bytes=64)
+        wos = keep.tile([P, 2, 1024], U8, name="wos", align_bytes=64)
+        wvq = keep.tile([P, 2, 1024], U32, name="wvq", align_bytes=64)
+        wvs = keep.tile([P, 2, 1024], U8, name="wvs", align_bytes=64)
+        xq = keep.tile([P, 4, 1024], U32, name="xq", align_bytes=64)
+        xs = keep.tile([P, 4, 1024], U8, name="xs", align_bytes=64)
+        dq = keep.tile([P, 4, 2, 512], U32, name="dq", align_bytes=64)
+        ds = keep.tile([P, 4, 2, 512], U8, name="ds", align_bytes=64)
+        tq = keep.tile([P, 4, 2, 512], U32, name="tq", align_bytes=64)
+        ts = keep.tile([P, 4, 2, 512], U8, name="ts", align_bytes=64)
+
+        live = {}
+
+        def move(e, out, in_):
+            if e == "V":
+                nc.vector.tensor_copy(out=out, in_=in_)
+            else:
+                nc.scalar.copy(out=out, in_=in_)
+
+        def big(key):
+            if key not in live:
+                live[key] = work.tile([P, 4, 1024], BF16, name="raw", bufs=6, align_bytes=64)
+            return live[key]
+
+        def stage(key):
+            if key not in live:
+                live[key] = work.tile([P, 512, 4], BF16, name="sx" if key[1] == "x" else "sw", bufs=3, align_bytes=64)
+            return live[key]
+
+        def interleave(e, dst, src):
+            move(
+                e,
+                dst.rearrange("p (c i) t -> p c t i", i=4),
+                src.rearrange("p t (c i) -> p c t i", i=4),
+            )
+
+        def quant(codes, scales, src, fmt):
+            nc.vector.quantize_mx(out=codes.bitcast(fmt), scales=scales, in_=src)
+
+        def emit(name, e):
+            k = name[:2]
+            if name[0] == "L":
+                if name == "Lpw":
+                    for i in range(4):
+                        nc.scalar.dma_start(out=pw[:, i], in_=pool_w[:, P * i : P * (i + 1), :].rearrange("s p h -> p s h"))
+                elif name[1:3] == "go":
+                    i = int(name[3])
+                    nc.sync.dma_start(out=go_raw[i][:], in_=grad_out[P * i : P * (i + 1), :])
+                elif name[1:3] == "Wo":
+                    b, g = int(name[3]), int(name[4])
+                    nc.sync.dma_start(
+                        out=big("Wo%d" % b)[:, :, 512 * g : 512 * g + 512],
+                        in_=Wo[512 * b : 512 * b + 512, 512 * g : 512 * g + 512].rearrange("(p j) c -> p j c", j=4),
+                    )
+                elif name[1:3] == "Wv":
+                    g = int(name[3])
+                    nc.sync.dma_start(out=big("Wv%d" % g)[:], in_=Wv[512 * g : 512 * g + 512, :].rearrange("(p j) c -> p j c", j=4))
+                else:
+                    i = int(name[2])
+                    nc.sync.dma_start(out=big("X%d" % i)[:], in_=values[:, P * i : P * (i + 1), :].rearrange("s p d -> p s d"))
+            elif k == "GT":
+                i = int(name[2])
+                ps = psum.tile([P, 4, P], F32, name="tt", bufs=2)
+                live["tg%d" % i] = ps
+                words = go_raw[i][:].bitcast(F32)
+                for b in range(2):
+                    for u in range(2):
+                        nc.tensor.transpose(ps[:, 2 * b + u, :], words[:, 256 * b + u : 256 * b + 256 : 2], ident[:])
+            elif k == "GC":
+                i = int(name[2])
+                ps = live["tg%d" % i]
+                gt = work.tile([P, 2, P, 4], BF16, name="got", bufs=2, align_bytes=64)
+                live["got%d" % i] = gt
+                out = gt[:].rearrange("p g b t -> p (g b t)").bitcast(F32).rearrange("p (g b u) -> p g b u", g=2, b=P)
+                move(e, out, ps[:].rearrange("p (g u) b -> p g b u", g=2))
+            elif k == "GQ":
+                i = int(name[2])
+                gt = live["got%d" % i]
+                quant(
+                    goq[:, i].rearrange("p g b -> p (g b)"),
+                    gos[:, i].rearrange("p g b -> p (g b)"),
+                    gt[:].rearrange("p g b t -> p (g b t)"),
+                    E5,
+                )
+            elif name[:3] == "WoI":
+                g, b, c = int(name[3]), int(name[4]), int(name[5])
+                st = stage("so%d%d" % (b, g))
+                interleave(e, st[:, 256 * c : 256 * c + 256, :], big("Wo%d" % b)[:, :, 512 * g + 256 * c : 512 * g + 256 * c + 256])
+            elif name[:3] == "WoQ":
+                g, b = int(name[3]), int(name[4])
+                cols = slice(512 * g, 512 * g + 512)
+                quant(woq[:, b, cols], wos[:, b, cols], stage("so%d%d" % (b, g))[:].rearrange("p c t -> p (c t)"), E4)
+            elif name[:3] == "WvI":
+                g, c = int(name[3]), int(name[4])
+                st = stage("sv%d%d" % (g, c // 2))
+                cc = 256 * (c % 2)
+                interleave(e, st[:, cc : cc + 256, :], big("Wv%d" % g)[:, :, 256 * c : 256 * c + 256])
+            elif name[:3] == "WvQ":
+                g, h = int(name[3]), int(name[4])
+                cols = slice(512 * h, 512 * h + 512)
+                quant(wvq[:, g, cols], wvs[:, g, cols], stage("sv%d%d" % (g, h))[:].rearrange("p c t -> p (c t)"), E4)
+            elif k == "XI":
+                i, c = int(name[2]), int(name[3])
+                st = stage("sx%d%d" % (i, c // 2))
+                cc = 256 * (c % 2)
+                interleave(e, st[:, cc : cc + 256, :], big("X%d" % i)[:, :, 256 * c : 256 * c + 256])
+            elif k == "XQ":
+                i, h = int(name[2]), int(name[3])
+                cols = slice(512 * h, 512 * h + 512)
+                quant(xq[:, i, cols], xs[:, i, cols], stage("sx%d%d" % (i, h))[:].rearrange("p c t -> p (c t)"), E4)
+            elif k == "DA":
+                i, g = int(name[2]), int(name[3])
+                ps = psum.tile([P, 512], F32, name="da", bufs=1)
+                live["da%d%d" % (i, g)] = ps
+                cols = slice(512 * g, 512 * g + 512)
+                for b in range(2):
+                    nc.tensor.matmul_mx(
+                        out=ps[:],
+                        lhsT=goq[:, i, b, :].bitcast(E5),
+                        lhsT_scale=gos[:, i, b, :],
+                        rhs=woq[:, b, cols].bitcast(E4),
+                        rhs_scale=wos[:, b, cols],
+                        start=(b == 0),
+                        stop=(b == 1),
+                    )
+            elif name[0] == "M":
+                i, g = int(name[1]), int(name[2])
+                ps = live["da%d%d" % (i, g)]
+                d = work.tile([P, 4, P, 4], BF16, name="dvp", bufs=5, align_bytes=64)
+                live["d%d%d" % (i, g)] = d
+                factor = pw[:, i, :, 8 * g : 8 * g + 8].rearrange("p s h -> p h s").unsqueeze(2).to_broadcast([P, 8, 16, 4])
+                for t in range(4):
+                    nc.vector.tensor_tensor(
+                        out=d[:, t].rearrange("p (h j) s -> p h j s", h=8),
+                        in0=ps[:].rearrange("p (h j t) -> p t h j", h=8, j=16)[:, t].unsqueeze(3).to_broadcast([P, 8, 16, 4]),
+                        in1=factor,
+                        op=MULT,
+                    )
+            elif k == "DQ":
+                i, g = int(name[2]), int(name[3])
+                quant(dq[:, i, g], ds[:, i, g], live["d%d%d" % (i, g)][:].rearrange("p t c s -> p (t c s)"), E5)
+            elif k == "TT":
+                i, g, u = int(name[2]), int(name[3]), int(name[4])
+                ps = psum.tile([P, 4, P], F32, name="tt", bufs=2)
+                live["tt%d%d%d" % (i, g, u)] = ps
+                words = live["d%d%d" % (i, g)][:].rearrange("p t c s -> p (t c s)").bitcast(F32)
+                for t in range(4):
+                    nc.tensor.transpose(ps[:, t, :], words[:, 256 * t + u : 256 * t + 256 : 2], ident[:])
+            elif k == "TC":
+                i, g, u = int(name[2]), int(name[3]), int(name[4])
+                ps = live["tt%d%d%d" % (i, g, u)]
+                key = "t%d%d" % (i, g)
+                if key not in live:
+                    live[key] = work.tile([P, 4, P, 4], BF16, name="dvt", bufs=3, align_bytes=64)
+                move(
+                    e,
+                    live[key][:, 2 * u : 2 * u + 2],
+                    ps[:].rearrange("p t b -> p (t b)").bitcast(BF16).rearrange("p (t b e) -> p e b t", t=4, b=P),
+                )
+            elif k == "TQ":
+                i, g = int(name[2]), int(name[3])
+                quant(tq[:, i, g], ts[:, i, g], live["t%d%d" % (i, g)][:].rearrange("p s b t -> p (s b t)"), E5)
+            elif k == "O1":
+                g, t, h, i = int(name[3]), int(name[4]), int(name[5]), int(name[6])
+                key = "a1%d%d%d" % (g, t, h)
+                if i == 0:
+                    live[key] = psum.tile([P, 512], F32, name="acc", bufs=5)
+                cols = slice(512 * h, 512 * h + 512)
+                m = slice(P * t, P * t + P)
+                nc.tensor.matmul_mx(
+                    out=live[key][:],
+                    lhsT=dq[:, i, g, m].bitcast(E5),
+                    lhsT_scale=ds[:, i, g, m],
+                    rhs=xq[:, i, cols].bitcast(E4),
+                    rhs_scale=xs[:, i, cols],
+                    start=(i == 0),
+                    stop=(i == 3),
+                )
+            elif k == "O0":
+                i, s, h = int(name[3]), int(name[4]), int(name[5])
+                ps = psum.tile([P, 512], F32, name="acc", bufs=5)
+                live["a0%d%d%d" % (i, s, h)] = ps
+                cols = slice(512 * h, 512 * h + 512)
+                m = slice(P * s, P * s + P)
+                for g in range(2):
+                    nc.tensor.matmul_mx(
+                        out=ps[:],
+                        lhsT=tq[:, i, g, m].bitcast(E5),
+                        lhsT_scale=ts[:, i, g, m],
+                        rhs=wvq[:, g, cols].bitcast(E4),
+                        rhs_scale=wvs[:, g, cols],
+                        start=(g == 0),
+                        stop=(g == 1),
+                    )
+            elif k == "E0" or k == "E1":
+                a, b, h = int(name[3]), int(name[4]), int(name[5])
+                key = "r%s%d%d" % (k, a, b)
+                if key not in live:
+                    live[key] = work.tile([P, 1024], F32, name="res" + k, bufs=4 if k == "E0" else 3)
+                move(e, live[key][:, 512 * h : 512 * h + 512], live["a%s%d%d%d" % (k[1], a, b, h)][:])
+            elif k == "S0":
+                i, s = int(name[3]), int(name[4])
+                nc.sync.dma_start(out=out_0[s, P * i : P * (i + 1), :], in_=live["rE0%d%d" % (i, s)][:])
+            elif k == "S1":
+                g, t = int(name[3]), int(name[4])
+                nc.sync.dma_start(
+                    out=out_1[512 * g : 512 * g + 512, :].rearrange("(p t) d -> p t d", t=4)[:, t, :],
+                    in_=live["rE1%d%d" % (g, t)][:],
+                )
+
+        with tc.manual_schedule():
+            for token in ORDER.split():
+                emit(token[:-2], token[-1])

@@ -14,32 +14,35 @@ E4 = mybir.dt.float8_e4m3fn_x4
 E5 = mybir.dt.float8_e5m2_x4
 MULT = mybir.AluOpType.mult
 P = 128
+SPAN = {"0": (0, 256), "1": (256, 256), "2": (512, 256), "3": (768, 256), "a": (0, 512), "b": (512, 512)}
 
 ORDER = """
-Lgo0:D LWo00:D GT0:P GC0:V LWo10:D WoI001:S WoI000:V GQ0:V LWo01:D WoI010:S WoI011:V WoQ00:V LWo11:D WoI100:S
-WoQ01:V Lpw:D WoI101:V DA00:P WoI110:S Lgo1:D WoQ10:V LX0:D GT1:P M00:V WoI111:S GC1:S LWv0:D XI00:S WoQ11:V
-TT000:P DQ00:V DA01:P TC000:S GQ1:V TT001:P XI01:V Lgo2:D M01:V XI02:S LWv1:D WvI00:S WvI01:V TT010:P TC001:S
-LX1:D WvI11:V WvQ00:V TC010:S TT011:P XQ00:V DA10:P XI03:S WvI02:V Lgo3:D GT2:P LX2:D WvI03:V GC2:S M10:V
-WvI10:S LX3:D XI10:S GQ2:V DA11:P XQ01:V XI11:S WvI12:V WvQ10:V TC011:S WvQ01:V TQ00:V XI12:S TT100:P TQ01:V
-GT3:P M11:V TC100:S O0_000:P XI21:S TT101:P XQ10:V DA20:P GC3:S WvI13:V TC101:S TT110:P DQ01:V WvQ11:V E0_000:S
-XI13:V XI22:S O0_001:P M20:V O0_010:P TC110:S O0_011:P TT111:P E0_001:S O0_020:P DQ10:V TC111:S DA21:P S0_00:D
-TQ10:V O0_021:P E0_010:S DQ11:V O0_030:P E0_011:S TQ11:V O0_031:P E0_020:S M21:V TT200:P S0_01:D E0_021:S
-TT201:P TC200:S S0_02:D O0_100:P XI23:S XQ11:V GQ3:V XI20:V E0_030:S DA30:P DQ20:V XI30:S O1_0000:P O1_0001:P
-M30:V TT210:P O0_101:P E0_031:S XI31:S DQ21:V E0_100:S DA31:P XQ20:V O0_110:P TC201:S DQ30:V O0_111:P XQ21:V
-TC210:S O1_0002:P TT211:P XQ30:V XI32:S TC211:V O1_0003:P O1_0010:P O1_0011:P TT300:P XI33:V E1_000:S O1_0012:P
-E0_101:S XQ31:V O0_120:P E0_110:S TQ20:V O0_121:P E0_111:S TC300:V O1_0013:P O1_0100:P E1_001:S O1_0101:P
-O1_0102:P E0_120:S M31:V O0_130:P S1_00:D E0_121:S O0_131:P O1_0103:P S0_03:D O1_0110:P TT301:P E1_010:V
-O1_0111:P S0_10:D E0_130:S TT310:P TQ21:V TC301:S O1_0112:P DQ31:V S0_11:D O1_0113:P O0_200:P TC310:V E0_131:S
-O1_0200:P O1_0201:P E0_200:S O1_0202:P E1_011:V O1_0203:P O1_0210:P E1_020:S O1_0211:P S1_01:D O1_0212:P
-O1_0213:P O0_201:P E1_021:S O0_210:P E0_201:S S1_02:D TT311:P O1_0300:P TC311:V O1_0301:P S0_12:D O1_0302:P
-O1_0303:P O1_0310:P E0_210:V E1_030:S O0_211:P S0_13:D O1_0311:P E0_211:S O1_0312:P O1_0313:P O0_220:P E1_031:V
-O1_1000:P E0_220:V O1_1001:P S1_03:D O0_221:P O1_1002:P E0_221:V O0_230:P S0_20:D O1_1003:P E0_230:V O1_1010:P
-O1_1011:P S0_21:D E1_100:V O0_231:P TQ30:V O1_1012:P O1_1013:P TQ31:V O1_1100:P E1_101:S O1_1101:P O1_1102:P
-E0_231:S O0_300:P S1_10:D O0_301:P E0_300:V O1_1103:P S0_22:D E0_301:S O1_1110:P E1_110:V O0_310:P O1_1111:P
-S0_23:D E0_310:S O0_311:P O1_1112:P E0_311:S O1_1113:P O1_1200:P E1_111:V O1_1201:P O0_320:P S1_11:D O1_1202:P
-E0_320:S O1_1203:P O1_1210:P E1_120:V O1_1211:P S0_30:D O1_1212:P O0_321:P O0_330:P S0_31:D E0_321:S O1_1213:P
-O0_331:P E1_121:S S0_32:D O1_1300:P E0_330:S O1_1301:P O1_1302:P E0_331:S O1_1303:P S1_12:D O1_1310:P E1_130:S
-O1_1311:P O1_1312:P O1_1313:P S0_33:D E1_131:S S1_13:D
+LWo00:D LWo10:D WoI000:V WoI001:S Lgo0:D WoI011:V WoI010:S Lgo1:D GT0:P WoQ00:V LWo01:D GT1:P GC0:S WoQ01:V
+Lpw:D GC1:S GQ0:V LWo11:D WoI100:S WoI101:V DA00:P GQ1:V LWv0:D M00:V WoI11a:S LWv1:D WoQ10:V WvI0a:S TT000:P
+WoQ11:V TT001:P DQ00:V DA01:P LX0:D WvI11:V WvI10:S M01:V TC000:S Lgo2:D Lgo3:D TC001:S LX1:D WvQ00:V DA10:P
+WvQ10:V GT2:P WvI13:S WvI0b:V TT010:P GC2:S M10:V TC010:S TT011:P TC011:S TQ00:V XI01:S TT100:P TQ01:V DA11:P
+WvQ01:V TC100:S GT3:P M11:V O0_000:P XI10:S O0_010:P O0_020:P GC3:S O0_030:P WvI12:V XI11:S TT101:P GQ2:V
+WvQ11:V E0_000:S DA20:P DQ01:V O0_001:P E0_010:S S0_000:D E0_030:V O0_011:P TC101:S S0_010:D M20:V TT110:P
+LX2:D E0_020:S O0_021:P TC110:S TT111:P XI00:V TC111:S DA21:P S0_020:D TQ10:V O0_031:P S0_030:D DQ10:V E0_001:S
+TT200:P E0_011:S TQ11:V S0_001:D E0_021:S DQ11:V LX3:D O0_100:P E0_031:S GQ3:V O0_110:P M21:V XI21:S O0_120:P
+O0_130:P TC200:S S0_011:D O0_101:P S0_021:D TT201:P XQ00:V E0_100:S S0_031:D TT210:P XI20:V E0_110:S S0_100:D
+DA30:P XQ10:V E0_120:S S0_110:D O0_111:P TC201:S DQ20:V S0_120:D O1_0000:P O1_0001:P XQ20:V TC210:S M30:V
+TT211:P O0_121:P E0_130:S TC211:S O0_131:P DQ21:V O1_0002:P XI31:S TT300:P XI30:V TT301:P DQ30:V E0_101:S
+DA31:P XQ30:V E0_111:S TQ20:V E0_121:S O1_0003:P O1_0100:P TQ21:V O1_0101:P E1_000:S O1_0102:P XI0b:V O1_0103:P
+E0_131:S O1_0200:P S1_000:D O1_0201:P XI22:S O1_0202:P S0_130:D O1_0203:P XI1b:V O0_200:P S0_101:D E1_010:S
+O1_0300:P O0_210:P E1_020:S XI23:V S1_010:D O1_0301:P E0_200:S O1_0302:P XQ01:V S0_111:D O0_220:P E0_210:S
+XQ11:V O1_0303:P S1_020:D O0_230:P XI3b:V E1_030:S S0_121:D O0_201:P E0_220:S S0_131:D O0_211:P E0_230:S XQ21:V
+S0_200:D O1_0010:P O0_221:P TC300:S XQ31:V S1_030:D O1_0011:P O1_0012:P M31:V O1_0013:P E0_201:S O1_0110:P
+O1_0111:P E0_211:S O1_0112:P O1_0113:P E1_001:S O1_0210:P O1_0211:P E1_011:S O1_0212:P S1_001:D O1_0213:P
+DQ31:V O1_0310:P S1_011:D E1_021:S O1_0311:P E0_221:V O1_0312:P S0_210:D O1_0313:P TC301:S O1_1000:P O1_1001:P
+S0_220:D O1_1002:P O1_1003:P E1_031:S S1_021:D O1_1100:P TQ30:V O1_1101:P E1_100:S O1_1102:P S1_031:D O1_1103:P
+O1_1200:P S0_230:D E1_110:S O1_1201:P O1_1202:P S0_201:D O1_1203:P O1_1300:P S0_211:D TT310:P S1_100:D TT311:P
+TC310:V S1_110:D O1_1301:P TC311:S O1_1302:P S0_221:D O1_1303:P O0_231:P E1_120:S O1_1010:P TQ31:V O1_1011:P
+E0_231:S O1_1012:P S1_120:D O1_1013:P E1_130:S O1_1110:P O1_1111:P E1_101:S O1_1112:P S1_130:D O0_300:P
+S1_101:D O0_310:P E0_300:S O1_1113:P S0_231:D E0_310:V O0_320:P E1_111:S S0_300:D O0_330:P E0_320:S S0_310:D
+O0_301:P E0_330:S O0_311:P S0_320:D E0_301:V O0_321:P S0_330:D E0_311:S O0_331:P S0_301:D E0_321:S O1_1210:P
+S1_111:D O1_1211:P E0_331:S O1_1212:P S0_311:D O1_1213:P O1_1310:P E1_121:S S0_321:D O1_1311:P O1_1312:P
+O1_1313:P S0_331:D E1_131:S S1_121:D S1_131:D
 """
 
 
@@ -82,7 +85,7 @@ def tile_multiheadattention_pb_v_kernel(tc, values, logw, Wv, Wo, pool_w, grad_o
 
         def stage(key):
             if key not in live:
-                live[key] = work.tile([P, 512, 4], BF16, name="sx" if key[1] == "x" else "sw", bufs=3, align_bytes=64)
+                live[key] = work.tile([P, 512, 4], BF16, name="sx" if key[1] == "x" else "sw", bufs=4 if key[1] == "x" else 3, align_bytes=64)
             return live[key]
 
         def interleave(e, dst, src):
@@ -141,27 +144,28 @@ def tile_multiheadattention_pb_v_kernel(tc, values, logw, Wv, Wo, pool_w, grad_o
                     E5,
                 )
             elif name[:3] == "WoI":
-                g, b, c = int(name[3]), int(name[4]), int(name[5])
+                g, b = int(name[3]), int(name[4])
+                c0, n = SPAN[name[5]]
                 st = stage("so%d%d" % (b, g))
-                interleave(e, st[:, 256 * c : 256 * c + 256, :], big("Wo%d" % b)[:, :, 512 * g + 256 * c : 512 * g + 256 * c + 256])
+                interleave(e, st[:, c0 : c0 + n, :], big("Wo%d" % b)[:, :, 512 * g + c0 : 512 * g + c0 + n])
             elif name[:3] == "WoQ":
                 g, b = int(name[3]), int(name[4])
                 cols = slice(512 * g, 512 * g + 512)
                 quant(woq[:, b, cols], wos[:, b, cols], stage("so%d%d" % (b, g))[:].rearrange("p c t -> p (c t)"), E4)
             elif name[:3] == "WvI":
-                g, c = int(name[3]), int(name[4])
-                st = stage("sv%d%d" % (g, c // 2))
-                cc = 256 * (c % 2)
-                interleave(e, st[:, cc : cc + 256, :], big("Wv%d" % g)[:, :, 256 * c : 256 * c + 256])
+                g = int(name[3])
+                c0, n = SPAN[name[4]]
+                st = stage("sv%d%d" % (g, c0 // 512))
+                interleave(e, st[:, c0 % 512 : c0 % 512 + n, :], big("Wv%d" % g)[:, :, c0 : c0 + n])
             elif name[:3] == "WvQ":
                 g, h = int(name[3]), int(name[4])
                 cols = slice(512 * h, 512 * h + 512)
                 quant(wvq[:, g, cols], wvs[:, g, cols], stage("sv%d%d" % (g, h))[:].rearrange("p c t -> p (c t)"), E4)
             elif k == "XI":
-                i, c = int(name[2]), int(name[3])
-                st = stage("sx%d%d" % (i, c // 2))
-                cc = 256 * (c % 2)
-                interleave(e, st[:, cc : cc + 256, :], big("X%d" % i)[:, :, 256 * c : 256 * c + 256])
+                i = int(name[2])
+                c0, n = SPAN[name[3]]
+                st = stage("sx%d%d" % (i, c0 // 512))
+                interleave(e, st[:, c0 % 512 : c0 % 512 + n, :], big("X%d" % i)[:, :, c0 : c0 + n])
             elif k == "XQ":
                 i, h = int(name[2]), int(name[3])
                 cols = slice(512 * h, 512 * h + 512)
@@ -252,18 +256,20 @@ def tile_multiheadattention_pb_v_kernel(tc, values, logw, Wv, Wo, pool_w, grad_o
                     )
             elif k == "E0" or k == "E1":
                 a, b, h = int(name[3]), int(name[4]), int(name[5])
-                key = "r%s%d%d" % (k, a, b)
-                if key not in live:
-                    live[key] = work.tile([P, 1024], F32, name="res" + k, bufs=4 if k == "E0" else 3)
-                move(e, live[key][:, 512 * h : 512 * h + 512], live["a%s%d%d%d" % (k[1], a, b, h)][:])
+                r = work.tile([P, 512], F32, name="r0" if k == "E0" else "r1", bufs=8 if k == "E0" else 4)
+                live["r%s%d%d%d" % (k[1], a, b, h)] = r
+                move(e, r[:], live["a%s%d%d%d" % (k[1], a, b, h)][:])
             elif k == "S0":
-                i, s = int(name[3]), int(name[4])
-                nc.sync.dma_start(out=out_0[s, P * i : P * (i + 1), :], in_=live["rE0%d%d" % (i, s)][:])
-            elif k == "S1":
-                g, t = int(name[3]), int(name[4])
+                i, s, h = int(name[3]), int(name[4]), int(name[5])
                 nc.sync.dma_start(
-                    out=out_1[512 * g : 512 * g + 512, :].rearrange("(p t) d -> p t d", t=4)[:, t, :],
-                    in_=live["rE1%d%d" % (g, t)][:],
+                    out=out_0[s, P * i : P * (i + 1), 512 * h : 512 * h + 512],
+                    in_=live["r0%d%d%d" % (i, s, h)][:],
+                )
+            elif k == "S1":
+                g, t, h = int(name[3]), int(name[4]), int(name[5])
+                nc.sync.dma_start(
+                    out=out_1[512 * g : 512 * g + 512, 512 * h : 512 * h + 512].rearrange("(p t) d -> p t d", t=4)[:, t, :],
+                    in_=live["r1%d%d%d" % (g, t, h)][:],
                 )
 
         with tc.manual_schedule():

from contextlib import ExitStack

import concourse.mybir as mybir
from concourse.masks import make_identity

FLOPS = 2 * 512 * 1024 * 1024 + 2 * 2 * 2048 * 1024 * 1024
BYTES = 2 * (4 * 512 * 1024 + 2 * 1024 * 1024 + 512 * 1024) + 4 * 4 * 512 * 16 + 4 * (2048 * 1024 + 1024 * 1024)

F32 = mybir.dt.float32
BF16 = mybir.dt.bfloat16
U32 = mybir.dt.uint32
U8 = mybir.dt.uint8
E4 = mybir.dt.float8_e4m3fn_x4
E5 = mybir.dt.float8_e5m2_x4
MULT = mybir.AluOpType.mult
P = 128
SPAN = {"0": (0, 256), "1": (256, 256), "2": (512, 256), "3": (768, 256), "a": (0, 512), "b": (512, 512)}

ORDER = """
LWo00:D LWo10:D WoI000:V WoI001:S Lgo0:D WoI011:V WoI010:S Lgo1:D GT0:P WoQ00:V LWo01:D GT1:P GC0:S WoQ01:V
Lpw:D GC1:S GQ0:V LWo11:D WoI100:S WoI101:V DA00:P GQ1:V LWv0:D M00:V WoI11a:S LWv1:D WoQ10:V WvI0a:S TT000:P
WoQ11:V TT001:P DQ00:V DA01:P LX0:D WvI11:V WvI10:S M01:V TC000:S Lgo2:D Lgo3:D TC001:S LX1:D WvQ00:V DA10:P
WvQ10:V GT2:P WvI13:S WvI0b:V TT010:P GC2:S M10:V TC010:S TT011:P TC011:S TQ00:V XI01:S TT100:P TQ01:V DA11:P
WvQ01:V TC100:S GT3:P M11:V O0_000:P XI10:S O0_010:P O0_020:P GC3:S O0_030:P WvI12:V XI11:S TT101:P GQ2:V
WvQ11:V E0_000:S DA20:P DQ01:V O0_001:P E0_010:S S0_000:D E0_030:V O0_011:P TC101:S S0_010:D M20:V TT110:P
LX2:D E0_020:S O0_021:P TC110:S TT111:P XI00:V TC111:S DA21:P S0_020:D TQ10:V O0_031:P S0_030:D DQ10:V E0_001:S
TT200:P E0_011:S TQ11:V S0_001:D E0_021:S DQ11:V LX3:D O0_100:P E0_031:S GQ3:V O0_110:P M21:V XI21:S O0_120:P
O0_130:P TC200:S S0_011:D O0_101:P S0_021:D TT201:P XQ00:V E0_100:S S0_031:D TT210:P XI20:V E0_110:S S0_100:D
DA30:P XQ10:V E0_120:S S0_110:D O0_111:P TC201:S DQ20:V S0_120:D O1_0000:P O1_0001:P XQ20:V TC210:S M30:V
TT211:P O0_121:P E0_130:S TC211:S O0_131:P DQ21:V O1_0002:P XI31:S TT300:P XI30:V TT301:P DQ30:V E0_101:S
DA31:P XQ30:V E0_111:S TQ20:V E0_121:S O1_0003:P O1_0100:P TQ21:V O1_0101:P E1_000:S O1_0102:P XI0b:V O1_0103:P
E0_131:S O1_0200:P S1_000:D O1_0201:P XI22:S O1_0202:P S0_130:D O1_0203:P XI1b:V O0_200:P S0_101:D E1_010:S
O1_0300:P O0_210:P E1_020:S XI23:V S1_010:D O1_0301:P E0_200:S O1_0302:P XQ01:V S0_111:D O0_220:P E0_210:S
XQ11:V O1_0303:P S1_020:D O0_230:P XI3b:V E1_030:S S0_121:D O0_201:P E0_220:S S0_131:D O0_211:P E0_230:S XQ21:V
S0_200:D O1_0010:P O0_221:P TC300:S XQ31:V S1_030:D O1_0011:P O1_0012:P M31:V O1_0013:P E0_201:S O1_0110:P
O1_0111:P E0_211:S O1_0112:P O1_0113:P E1_001:S O1_0210:P O1_0211:P E1_011:S O1_0212:P S1_001:D O1_0213:P
DQ31:V O1_0310:P S1_011:D E1_021:S O1_0311:P E0_221:V O1_0312:P S0_210:D O1_0313:P TC301:S O1_1000:P O1_1001:P
S0_220:D O1_1002:P O1_1003:P E1_031:S S1_021:D O1_1100:P TQ30:V O1_1101:P E1_100:S O1_1102:P S1_031:D O1_1103:P
O1_1200:P S0_230:D E1_110:S O1_1201:P O1_1202:P S0_201:D O1_1203:P O1_1300:P S0_211:D TT310:P S1_100:D TT311:P
TC310:V S1_110:D O1_1301:P TC311:S O1_1302:P S0_221:D O1_1303:P O0_231:P E1_120:S O1_1010:P TQ31:V O1_1011:P
E0_231:S O1_1012:P S1_120:D O1_1013:P E1_130:S O1_1110:P O1_1111:P E1_101:S O1_1112:P S1_130:D O0_300:P
S1_101:D O0_310:P E0_300:S O1_1113:P S0_231:D E0_310:V O0_320:P E1_111:S S0_300:D O0_330:P E0_320:S S0_310:D
O0_301:P E0_330:S O0_311:P S0_320:D E0_301:V O0_321:P S0_330:D E0_311:S O0_331:P S0_301:D E0_321:S O1_1210:P
S1_111:D O1_1211:P E0_331:S O1_1212:P S0_311:D O1_1213:P O1_1310:P E1_121:S S0_321:D O1_1311:P O1_1312:P
O1_1313:P S0_331:D E1_131:S S1_121:D S1_131:D
"""


def tile_multiheadattention_pb_v_kernel(tc, values, logw, Wv, Wo, pool_w, grad_out, out_0, out_1):
    nc = tc.nc
    with ExitStack() as ctx:
        keep = ctx.enter_context(tc.tile_pool(name="keep", bufs=1))
        work = ctx.enter_context(tc.tile_pool(name="work", bufs=1))
        psum = ctx.enter_context(tc.psum_pool(name="psum", bufs=1))

        ident = keep.tile([P, P], F32, name="ident")
        make_identity(nc, ident[:])
        pw = keep.tile([P, 4, 4, 16], F32, name="pw")
        go_raw = [keep.tile([P, 1024], BF16, name="go_raw%d" % i) for i in range(4)]
        goq = keep.tile([P, 4, 2, P], U32, name="goq", align_bytes=64)
        gos = keep.tile([P, 4, 2, P], U8, name="gos", align_bytes=64)
        woq = keep.tile([P, 2, 1024], U32, name="woq", align_bytes=64)
        wos = keep.tile([P, 2, 1024], U8, name="wos", align_bytes=64)
        wvq = keep.tile([P, 2, 1024], U32, name="wvq", align_bytes=64)
        wvs = keep.tile([P, 2, 1024], U8, name="wvs", align_bytes=64)
        xq = keep.tile([P, 4, 1024], U32, name="xq", align_bytes=64)
        xs = keep.tile([P, 4, 1024], U8, name="xs", align_bytes=64)
        dq = keep.tile([P, 4, 2, 512], U32, name="dq", align_bytes=64)
        ds = keep.tile([P, 4, 2, 512], U8, name="ds", align_bytes=64)
        tq = keep.tile([P, 4, 2, 512], U32, name="tq", align_bytes=64)
        ts = keep.tile([P, 4, 2, 512], U8, name="ts", align_bytes=64)

        live = {}

        def move(e, out, in_):
            if e == "V":
                nc.vector.tensor_copy(out=out, in_=in_)
            else:
                nc.scalar.copy(out=out, in_=in_)

        def big(key):
            if key not in live:
                live[key] = work.tile([P, 4, 1024], BF16, name="raw", bufs=6, align_bytes=64)
            return live[key]

        def stage(key):
            if key not in live:
                live[key] = work.tile([P, 512, 4], BF16, name="sx" if key[1] == "x" else "sw", bufs=4 if key[1] == "x" else 3, align_bytes=64)
            return live[key]

        def interleave(e, dst, src):
            move(
                e,
                dst.rearrange("p (c i) t -> p c t i", i=4),
                src.rearrange("p t (c i) -> p c t i", i=4),
            )

        def quant(codes, scales, src, fmt):
            nc.vector.quantize_mx(out=codes.bitcast(fmt), scales=scales, in_=src)

        def emit(name, e):
            k = name[:2]
            if name[0] == "L":
                if name == "Lpw":
                    for i in range(4):
                        nc.scalar.dma_start(out=pw[:, i], in_=pool_w[:, P * i : P * (i + 1), :].rearrange("s p h -> p s h"))
                elif name[1:3] == "go":
                    i = int(name[3])
                    nc.sync.dma_start(out=go_raw[i][:], in_=grad_out[P * i : P * (i + 1), :])
                elif name[1:3] == "Wo":
                    b, g = int(name[3]), int(name[4])
                    nc.sync.dma_start(
                        out=big("Wo%d" % b)[:, :, 512 * g : 512 * g + 512],
                        in_=Wo[512 * b : 512 * b + 512, 512 * g : 512 * g + 512].rearrange("(p j) c -> p j c", j=4),
                    )
                elif name[1:3] == "Wv":
                    g = int(name[3])
                    nc.sync.dma_start(out=big("Wv%d" % g)[:], in_=Wv[512 * g : 512 * g + 512, :].rearrange("(p j) c -> p j c", j=4))
                else:
                    i = int(name[2])
                    nc.sync.dma_start(out=big("X%d" % i)[:], in_=values[:, P * i : P * (i + 1), :].rearrange("s p d -> p s d"))
            elif k == "GT":
                i = int(name[2])
                ps = psum.tile([P, 4, P], F32, name="tt", bufs=2)
                live["tg%d" % i] = ps
                words = go_raw[i][:].bitcast(F32)
                for b in range(2):
                    for u in range(2):
                        nc.tensor.transpose(ps[:, 2 * b + u, :], words[:, 256 * b + u : 256 * b + 256 : 2], ident[:])
            elif k == "GC":
                i = int(name[2])
                ps = live["tg%d" % i]
                gt = work.tile([P, 2, P, 4], BF16, name="got", bufs=2, align_bytes=64)
                live["got%d" % i] = gt
                out = gt[:].rearrange("p g b t -> p (g b t)").bitcast(F32).rearrange("p (g b u) -> p g b u", g=2, b=P)
                move(e, out, ps[:].rearrange("p (g u) b -> p g b u", g=2))
            elif k == "GQ":
                i = int(name[2])
                gt = live["got%d" % i]
                quant(
                    goq[:, i].rearrange("p g b -> p (g b)"),
                    gos[:, i].rearrange("p g b -> p (g b)"),
                    gt[:].rearrange("p g b t -> p (g b t)"),
                    E5,
                )
            elif name[:3] == "WoI":
                g, b = int(name[3]), int(name[4])
                c0, n = SPAN[name[5]]
                st = stage("so%d%d" % (b, g))
                interleave(e, st[:, c0 : c0 + n, :], big("Wo%d" % b)[:, :, 512 * g + c0 : 512 * g + c0 + n])
            elif name[:3] == "WoQ":
                g, b = int(name[3]), int(name[4])
                cols = slice(512 * g, 512 * g + 512)
                quant(woq[:, b, cols], wos[:, b, cols], stage("so%d%d" % (b, g))[:].rearrange("p c t -> p (c t)"), E4)
            elif name[:3] == "WvI":
                g = int(name[3])
                c0, n = SPAN[name[4]]
                st = stage("sv%d%d" % (g, c0 // 512))
                interleave(e, st[:, c0 % 512 : c0 % 512 + n, :], big("Wv%d" % g)[:, :, c0 : c0 + n])
            elif name[:3] == "WvQ":
                g, h = int(name[3]), int(name[4])
                cols = slice(512 * h, 512 * h + 512)
                quant(wvq[:, g, cols], wvs[:, g, cols], stage("sv%d%d" % (g, h))[:].rearrange("p c t -> p (c t)"), E4)
            elif k == "XI":
                i = int(name[2])
                c0, n = SPAN[name[3]]
                st = stage("sx%d%d" % (i, c0 // 512))
                interleave(e, st[:, c0 % 512 : c0 % 512 + n, :], big("X%d" % i)[:, :, c0 : c0 + n])
            elif k == "XQ":
                i, h = int(name[2]), int(name[3])
                cols = slice(512 * h, 512 * h + 512)
                quant(xq[:, i, cols], xs[:, i, cols], stage("sx%d%d" % (i, h))[:].rearrange("p c t -> p (c t)"), E4)
            elif k == "DA":
                i, g = int(name[2]), int(name[3])
                ps = psum.tile([P, 512], F32, name="da", bufs=1)
                live["da%d%d" % (i, g)] = ps
                cols = slice(512 * g, 512 * g + 512)
                for b in range(2):
                    nc.tensor.matmul_mx(
                        out=ps[:],
                        lhsT=goq[:, i, b, :].bitcast(E5),
                        lhsT_scale=gos[:, i, b, :],
                        rhs=woq[:, b, cols].bitcast(E4),
                        rhs_scale=wos[:, b, cols],
                        start=(b == 0),
                        stop=(b == 1),
                    )
            elif name[0] == "M":
                i, g = int(name[1]), int(name[2])
                ps = live["da%d%d" % (i, g)]
                d = work.tile([P, 4, P, 4], BF16, name="dvp", bufs=5, align_bytes=64)
                live["d%d%d" % (i, g)] = d
                factor = pw[:, i, :, 8 * g : 8 * g + 8].rearrange("p s h -> p h s").unsqueeze(2).to_broadcast([P, 8, 16, 4])
                for t in range(4):
                    nc.vector.tensor_tensor(
                        out=d[:, t].rearrange("p (h j) s -> p h j s", h=8),
                        in0=ps[:].rearrange("p (h j t) -> p t h j", h=8, j=16)[:, t].unsqueeze(3).to_broadcast([P, 8, 16, 4]),
                        in1=factor,
                        op=MULT,
                    )
            elif k == "DQ":
                i, g = int(name[2]), int(name[3])
                quant(dq[:, i, g], ds[:, i, g], live["d%d%d" % (i, g)][:].rearrange("p t c s -> p (t c s)"), E5)
            elif k == "TT":
                i, g, u = int(name[2]), int(name[3]), int(name[4])
                ps = psum.tile([P, 4, P], F32, name="tt", bufs=2)
                live["tt%d%d%d" % (i, g, u)] = ps
                words = live["d%d%d" % (i, g)][:].rearrange("p t c s -> p (t c s)").bitcast(F32)
                for t in range(4):
                    nc.tensor.transpose(ps[:, t, :], words[:, 256 * t + u : 256 * t + 256 : 2], ident[:])
            elif k == "TC":
                i, g, u = int(name[2]), int(name[3]), int(name[4])
                ps = live["tt%d%d%d" % (i, g, u)]
                key = "t%d%d" % (i, g)
                if key not in live:
                    live[key] = work.tile([P, 4, P, 4], BF16, name="dvt", bufs=3, align_bytes=64)
                move(
                    e,
                    live[key][:, 2 * u : 2 * u + 2],
                    ps[:].rearrange("p t b -> p (t b)").bitcast(BF16).rearrange("p (t b e) -> p e b t", t=4, b=P),
                )
            elif k == "TQ":
                i, g = int(name[2]), int(name[3])
                quant(tq[:, i, g], ts[:, i, g], live["t%d%d" % (i, g)][:].rearrange("p s b t -> p (s b t)"), E5)
            elif k == "O1":
                g, t, h, i = int(name[3]), int(name[4]), int(name[5]), int(name[6])
                key = "a1%d%d%d" % (g, t, h)
                if i == 0:
                    live[key] = psum.tile([P, 512], F32, name="acc", bufs=5)
                cols = slice(512 * h, 512 * h + 512)
                m = slice(P * t, P * t + P)
                nc.tensor.matmul_mx(
                    out=live[key][:],
                    lhsT=dq[:, i, g, m].bitcast(E5),
                    lhsT_scale=ds[:, i, g, m],
                    rhs=xq[:, i, cols].bitcast(E4),
                    rhs_scale=xs[:, i, cols],
                    start=(i == 0),
                    stop=(i == 3),
                )
            elif k == "O0":
                i, s, h = int(name[3]), int(name[4]), int(name[5])
                ps = psum.tile([P, 512], F32, name="acc", bufs=5)
                live["a0%d%d%d" % (i, s, h)] = ps
                cols = slice(512 * h, 512 * h + 512)
                m = slice(P * s, P * s + P)
                for g in range(2):
                    nc.tensor.matmul_mx(
                        out=ps[:],
                        lhsT=tq[:, i, g, m].bitcast(E5),
                        lhsT_scale=ts[:, i, g, m],
                        rhs=wvq[:, g, cols].bitcast(E4),
                        rhs_scale=wvs[:, g, cols],
                        start=(g == 0),
                        stop=(g == 1),
                    )
            elif k == "E0" or k == "E1":
                a, b, h = int(name[3]), int(name[4]), int(name[5])
                r = work.tile([P, 512], F32, name="r0" if k == "E0" else "r1", bufs=8 if k == "E0" else 4)
                live["r%s%d%d%d" % (k[1], a, b, h)] = r
                move(e, r[:], live["a%s%d%d%d" % (k[1], a, b, h)][:])
            elif k == "S0":
                i, s, h = int(name[3]), int(name[4]), int(name[5])
                nc.sync.dma_start(
                    out=out_0[s, P * i : P * (i + 1), 512 * h : 512 * h + 512],
                    in_=live["r0%d%d%d" % (i, s, h)][:],
                )
            elif k == "S1":
                g, t, h = int(name[3]), int(name[4]), int(name[5])
                nc.sync.dma_start(
                    out=out_1[512 * g : 512 * g + 512, 512 * h : 512 * h + 512].rearrange("(p t) d -> p t d", t=4)[:, t, :],
                    in_=live["r1%d%d%d" % (g, t, h)][:],
                )

        with tc.manual_schedule():
            for token in ORDER.split():
                emit(token[:-2], token[-1])
